import numpy as np
import ml_dtypes


def mxq(x, axis, fmt="e4m3"):
    dtype, down = {"e4m3": (ml_dtypes.float8_e4m3fn, 7), "e5m2": (ml_dtypes.float8_e5m2, 14)}[fmt]
    v = np.moveaxis(np.asarray(x, np.float32).astype(ml_dtypes.bfloat16).astype(np.float64), axis, -1)
    blocks = v.reshape(v.shape[:-1] + (-1, 32))
    amax = np.abs(blocks).max(-1, keepdims=True)
    byte = np.maximum(np.where(amax > 0, np.frexp(amax)[1] - 1 + 127, 0) - down, 1)
    scale = np.exp2(byte - 127.0)
    codes = (blocks / scale).astype(np.float32).astype(dtype).astype(np.float64)
    return np.moveaxis((codes * scale).reshape(v.shape), -1, axis)


WIDE = False


def mx_kscale(k):
    if not WIDE:
        return np.ones(k)
    levels = np.array([30, -30])
    if k % 512:
        return np.exp2(np.random.permutation(np.resize(levels, k // 32))).repeat(32)
    a = np.empty((k // 512, 16))
    for p in range(k // 512):
        a[p, :8] = np.random.permutation(np.resize(levels, 8))
        for g in range(8):
            far = levels[np.abs(levels - a[p, g]) >= 10]
            a[p, g + 8] = far[np.random.randint(len(far))]
    return np.exp2(a.ravel()).repeat(32)


BF16 = ml_dtypes.bfloat16


def bf(x):
    return np.asarray(x, np.float32).astype(BF16)


def f64(x):
    return np.asarray(x).astype(np.float64)


B, L, D, H, G, DH = 1, 512, 2560, 16, 8, 128
HALF = DH // 2
ROPE_THETA = 10000.0
SCALE = 1.0 / np.sqrt(144.0)


def rope_cos_sin():
    inv_freq = 1.0 / ROPE_THETA ** (np.arange(0, DH, 2) / DH)
    ang = np.arange(L)[:, None] * inv_freq[None, :]
    return np.cos(ang), np.sin(ang)


def apply_rope(t, cos, sin):
    t1, t2 = t[..., :HALF], t[..., HALF:]
    c, s = cos[None, None, :, :], sin[None, None, :, :]
    return np.concatenate([t1 * c - t2 * s, t2 * c + t1 * s], axis=-1)


def heads(y, n):
    return y.reshape(B, L, n, DH).transpose(0, 2, 1, 3)


def setup_inputs():
    s = mx_kscale(D)
    return {"x": bf(np.random.standard_normal((B, L, D)) * s),
            "wq": bf(np.random.standard_normal((H * DH, D)) * 2.0 / np.sqrt(D) / s[None, :]),
            "wk": bf(np.random.standard_normal((G * DH, D)) * 1.5 / np.sqrt(D) / s[None, :]),
            "wv": bf(np.random.standard_normal((G * DH, D)) * 1.0 / np.sqrt(D) / s[None, :])}


def reference(x, wq, wk, wv):
    xq = mxq(f64(x), 2, "e5m2")
    q = heads(xq @ mxq(f64(wq), 1, "e4m3").T, H)
    k = heads(xq @ mxq(f64(wk), 1, "e4m3").T, G)
    v = heads(xq @ mxq(f64(wv), 1, "e4m3").T, G)
    cos, sin = rope_cos_sin()
    return apply_rope(q, cos, sin) * SCALE, apply_rope(k, cos, sin), v

@@ -1,0 +1,233 @@
+import math
+from contextlib import ExitStack
+
+import concourse.mybir as mybir
+from concourse.masks import make_identity
+
+L, D, H, G, DH = 512, 2560, 16, 8, 128
+HALF = DH // 2
+ROPE_THETA = 10000.0
+Q_SCALE = 1.0 / math.sqrt(144.0)
+FLOPS = 2 * L * D * (H + 2 * G) * DH
+
+F32 = mybir.dt.float32
+BF16 = mybir.dt.bfloat16
+I32 = mybir.dt.int32
+U32 = mybir.dt.uint32
+U8 = mybir.dt.uint8
+E4M3 = mybir.dt.float8_e4m3fn_x4
+E5M2 = mybir.dt.float8_e5m2_x4
+ALU = mybir.AluOpType
+ACT = mybir.ActivationFunctionType
+
+P = 128
+K_PASS = 512
+PASSES = D // K_PASS
+WORDS = K_PASS // 2
+SLAB = 256
+TOK = L // P
+CHUNKS = ((0, 3), (3, 5))
+QUANT = ((0, 2), (2, 4), (4, 5))
+HEAD_SLABS = 4
+SORTED_BY_SCALAR = 4
+
+
+def tile_attention_pa_kernel(tc, x, wq, wk, wv, out_0, out_1, out_2):
+    nc = tc.nc
+    x_rows = x[0].rearrange("(p j) k -> p j k", j=TOK)
+
+    def weight_slabs(w, out, table, first, last):
+        return [(w[SLAB * m : SLAB * (m + 1), :].rearrange("(r p) k -> p r k", p=P),
+                 out[0, 2 * m : 2 * m + 2].rearrange("h (p j) d -> p h (j d)", j=TOK), table)
+                for m in range(first, last)]
+
+    v_slabs = G // 2
+    steps = (weight_slabs(wv, out_2, None, 0, v_slabs - 1) + weight_slabs(wq, out_0, "q", 0, H // 2)
+             + weight_slabs(wk, out_1, "k", 0, G // 2) + weight_slabs(wv, out_2, None, v_slabs - 1, v_slabs))
+    n_steps = len(steps)
+    sources = [x_rows[:, 0:2, :], x_rows[:, 2:4, :]] + [s[0] for s in steps]
+    n_slabs = len(sources)
+
+    with ExitStack() as ctx:
+        const = ctx.enter_context(tc.tile_pool(name="const", bufs=1))
+        work = ctx.enter_context(tc.tile_pool(name="work", bufs=3))
+        psum = ctx.enter_context(tc.psum_pool(name="psum", bufs=1))
+        ctx.enter_context(tc.manual_schedule())
+
+        raw, ordered, banks, grouped, codes, scales, accs, prods, staged = {}, {}, {}, {}, {}, {}, {}, {}, {}
+
+        def load(s):
+            for c, (g0, g1) in enumerate(CHUNKS):
+                rows = work.tile([P, 2, (g1 - g0) * K_PASS], BF16, name="rows%d" % c, bufs=4, align_bytes=64)
+                nc.sync.dma_start(out=rows[:], in_=sources[s][:, :, g0 * K_PASS : g1 * K_PASS])
+                raw[s, c] = rows[:].rearrange("q r k -> q (r k)").bitcast(F32).rearrange("q (r w) -> q r w", r=2)
+
+        def sort_words(s, copy, n_passes):
+            for c, (g0, g1) in enumerate(CHUNKS):
+                n = min(g1, n_passes) - g0
+                srt = work.tile([P, 2, 2, (g1 - g0) * P], F32, name="sorted%d" % c, bufs=2, align_bytes=64)
+                copy(out=srt[:, :, :, : n * P],
+                     in_=raw[s, c][:, :, : n * WORDS].rearrange("q r (w u) -> q r u w", u=2))
+                for g in range(g0, g0 + n):
+                    ordered[s, g] = srt[:, :, :, (g - g0) * P : (g - g0 + 1) * P]
+
+        def transposes(s):
+            for c, (g0, g1) in enumerate(CHUNKS):
+                for g in range(g0, g1):
+                    bank = psum.tile([P, 2, 2, P], F32, name="turned", bufs=5)
+                    for r in range(2):
+                        for u in range(2):
+                            if (s, g) in ordered:
+                                src = ordered[s, g][:, r, u, :]
+                            else:
+                                src = raw[s, c][:, r, (g - g0) * WORDS + u : (g - g0 + 1) * WORDS : 2]
+                            nc.tensor.transpose(bank[:, r, u, :], src, ident[:])
+                    banks[s, g] = bank
+
+        def gather(s, g, copy):
+            if g == 0:
+                grouped[s] = work.tile([P, PASSES, 4 * SLAB], BF16, name="grouped", bufs=2, align_bytes=64)
+            words = grouped[s][:, g, :].bitcast(F32).rearrange("q (r c u) -> q r c u", r=2, u=2)
+            copy(out=words, in_=banks[s, g][:].rearrange("q r u c -> q r c u"))
+
+        def quantise(s, part):
+            is_x = s < 2
+            if part == 0:
+                tag = "x" if is_x else "w"
+                codes[s] = work.tile([P, PASSES, SLAB], U32, name=tag + "_codes", bufs=2 if is_x else 3, align_bytes=64)
+                scales[s] = work.tile([P, PASSES, SLAB], U8, name=tag + "_scales", bufs=2 if is_x else 3, align_bytes=64)
+            g0, g1 = QUANT[part]
+            nc.vector.quantize_mx(
+                out=codes[s][:, g0:g1, :].rearrange("q g c -> q (g c)").bitcast(E5M2 if is_x else E4M3),
+                scales=scales[s][:, g0:g1, :].rearrange("q g c -> q (g c)"),
+                in_=grouped[s][:, g0:g1, :].rearrange("q g c -> q (g c)"))
+
+        def matmuls(n):
+            for jp in range(2):
+                acc = psum.tile([P, 2 * SLAB], F32, name="acc", bufs=3)
+                for j in range(2):
+                    for g in range(PASSES):
+                        nc.tensor.matmul_mx(
+                            out=acc[:, j * SLAB : (j + 1) * SLAB],
+                            lhsT=codes[jp][:, g, j * P : (j + 1) * P].bitcast(E5M2),
+                            lhsT_scale=scales[jp][:, g, j * P : (j + 1) * P],
+                            rhs=codes[n + 2][:, g, :].bitcast(E4M3),
+                            rhs_scale=scales[n + 2][:, g, :],
+                            start=(g == 0), stop=(g == PASSES - 1))
+                accs[n, jp] = acc
+
+        def stage_tile(n):
+            if n not in staged:
+                staged[n] = work.tile([P, 2, TOK, DH], F32, name="staged", bufs=4)
+            return staged[n]
+
+        def copy_out(n, jp):
+            nc.scalar.copy(out=stage_tile(n)[:, :, 2 * jp : 2 * jp + 2, :].rearrange("q h j d -> q j h d"),
+                           in_=accs[n, jp][:].rearrange("q (j h d) -> q j h d", j=2, h=2))
+
+        def rope_products(n, jp):
+            shape = [P, 2, 2, 4, HALF]
+            prod = work.tile(shape, F32, name="prod", bufs=3)
+            nc.vector.tensor_tensor(
+                out=prod[:],
+                in0=accs[n, jp][:].rearrange("q (o j a i) -> q o j a i", o=1, j=2, a=4).to_broadcast(shape),
+                in1=tables[steps[n][2]][:, jp].rearrange("q c j (o i) -> q c j o i", o=1).to_broadcast(shape),
+                op=ALU.mult)
+            prods[n, jp] = prod
+
+        def rope_sums(n, jp):
+            dst = stage_tile(n)[:, :, 2 * jp : 2 * jp + 2, :].rearrange("q h j (a i) -> q j h a i", a=2)
+            prod = prods[n, jp][:].rearrange("q c j (h a) i -> q c j h a i", a=2)
+            nc.vector.tensor_tensor(out=dst[:, :, :, 0, :], in0=prod[:, 0, :, :, 0, :], in1=prod[:, 1, :, :, 1, :],
+                                    op=ALU.subtract)
+            nc.vector.tensor_tensor(out=dst[:, :, :, 1, :], in0=prod[:, 0, :, :, 1, :], in1=prod[:, 1, :, :, 0, :],
+                                    op=ALU.add)
+
+        def store(n, j0, j1):
+            nc.sync.dma_start(out=steps[n][1][:, :, j0 * DH : j1 * DH],
+                              in_=staged[n][:, :, j0:j1, :].rearrange("q h j d -> q h (j d)"))
+
+        def is_rope(n):
+            return 0 <= n < n_steps and steps[n][2] is not None
+
+        for s in range(HEAD_SLABS):
+            load(s)
+
+        ident = const.tile([P, P], F32)
+        pos = const.tile([P, TOK], F32)
+        nc.gpsimd.iota(pos[:], [[1, TOK]], base=0, channel_multiplier=TOK, allow_small_or_imprecise_dtypes=True)
+        make_identity(nc, ident[:])
+
+        turns = const.tile([P, 2, 2, 2, HALF], F32)
+        ratio = ROPE_THETA ** (-1.0 / HALF)
+        pos_view = pos[:].rearrange("q (t j o) -> q t j o", t=2, o=1)
+        for i in range(8):
+            nc.vector.tensor_scalar(out=turns[:, :, 1, :, i : i + 1], in0=pos_view,
+                                    scalar1=ratio**i / (2.0 * math.pi), scalar2=None, op0=ALU.mult)
+        for b in range(1, 8):
+            nc.vector.tensor_scalar(out=turns[:, :, 1, :, 8 * b : 8 * b + 8], in0=turns[:, :, 1, :, 0:8],
+                                    scalar1=ratio ** (8 * b), scalar2=None, op0=ALU.mult)
+        nc.vector.tensor_scalar(out=turns[:, :, 0, :, :], in0=turns[:, :, 1, :, :],
+                                scalar1=0.25, scalar2=None, op0=ALU.add)
+        flat = "q t c j i -> q (t c j i)"
+        whole = const.tile([P, 8 * HALF], I32)
+        nc.vector.tensor_copy(out=whole[:], in_=turns[:].rearrange(flat))
+        rest = const.tile([P, 8 * HALF], F32)
+        nc.vector.tensor_tensor(out=rest[:], in0=turns[:].rearrange(flat), in1=whole[:], op=ALU.subtract)
+        table_k = const.tile([P, 2, 2, 2, HALF], F32)
+        table_q = const.tile([P, 2, 2, 2, HALF], F32)
+        nc.scalar.activation(out=table_k[:].rearrange(flat), in_=rest[:], func=ACT.Sin, scale=2.0 * math.pi)
+        tables = {"q": table_q, "k": table_k}
+
+        def head_slab(s):
+            transposes(s)
+            for g in range(PASSES):
+                gather(s, g, nc.vector.tensor_copy if g % 2 else nc.scalar.copy)
+            for part in range(len(QUANT)):
+                quantise(s, part)
+
+        for s in range(3):
+            head_slab(s)
+            load(s + HEAD_SLABS)
+            if s == 0:
+                nc.vector.tensor_scalar(out=table_q[:].rearrange(flat), in0=table_k[:].rearrange(flat),
+                                        scalar1=Q_SCALE, scalar2=None, op0=ALU.mult)
+
+        for n in range(n_steps):
+            s = n + 3
+            more = s < n_slabs
+            if more:
+                transposes(s)
+            if n > 0:
+                if is_rope(n - 1):
+                    rope_products(n - 1, 1)
+                    rope_sums(n - 1, 0)
+                else:
+                    copy_out(n - 1, 1)
+            if more:
+                for g in range(PASSES):
+                    gather(s, g, nc.vector.tensor_copy if s < HEAD_SLABS and g % 2 else nc.scalar.copy)
+                quantise(s, 0)
+            if is_rope(n - 1):
+                rope_sums(n - 1, 1)
+            if n > 0:
+                store(n - 1, 0, TOK)
+            if s + HEAD_SLABS < n_slabs:
+                load(s + HEAD_SLABS)
+            if more:
+                quantise(s, 1)
+                quantise(s, 2)
+            matmuls(n)
+            if is_rope(n):
+                rope_products(n, 0)
+            else:
+                copy_out(n, 0)
+            if s + 1 < n_slabs:
+                if is_rope(n - 1):
+                    sort_words(s + 1, nc.scalar.copy, SORTED_BY_SCALAR)
+                else:
+                    sort_words(s + 1, nc.vector.tensor_copy, PASSES)
+        last = n_steps - 1
+        store(last, 0, 2)
+        copy_out(last, 1)
+        store(last, 2, TOK)

@@ -29,6 +29,7 @@ TOK = L // P
 CHUNKS = ((0, 3), (3, 5))
 QUANT = ((0, 2), (2, 4), (4, 5))
 HEAD_SLABS = 4
+ROW_BUFS = 5
 SORTED_BY_SCALAR = 4
 
 
@@ -42,10 +43,12 @@ def tile_attention_pa_kernel(tc, x, wq, wk, wv, out_0, out_1, out_2):
                 for m in range(first, last)]
 
     v_slabs = G // 2
-    steps = (weight_slabs(wv, out_2, None, 0, v_slabs - 1) + weight_slabs(wq, out_0, "q", 0, H // 2)
-             + weight_slabs(wk, out_1, "k", 0, G // 2) + weight_slabs(wv, out_2, None, v_slabs - 1, v_slabs))
+    steps = (weight_slabs(wv, out_2, None, 0, v_slabs // 2) + weight_slabs(wq, out_0, "q", 0, H // 2)
+             + weight_slabs(wk, out_1, "k", 0, G // 2) + weight_slabs(wv, out_2, None, v_slabs // 2, v_slabs))
     n_steps = len(steps)
-    sources = [x_rows[:, 0:2, :], x_rows[:, 2:4, :]] + [s[0] for s in steps]
+    sources = [x_rows[:, 0:2, :], steps[0][0], x_rows[:, 2:4, :]] + [step[0] for step in steps[1:]]
+    x_slab = {0: 0, 1: 0, 2: 2, 3: 2}
+    w_slab = [1] + list(range(3, n_steps + 2))
     n_slabs = len(sources)
 
     with ExitStack() as ctx:
@@ -58,14 +61,16 @@ def tile_attention_pa_kernel(tc, x, wq, wk, wv, out_0, out_1, out_2):
 
         def load(s):
             for c, (g0, g1) in enumerate(CHUNKS):
-                rows = work.tile([P, 2, (g1 - g0) * K_PASS], BF16, name="rows%d" % c, bufs=4, align_bytes=64)
+                rows = work.tile([P, 2, (g1 - g0) * K_PASS], BF16, name="rows%d" % c, bufs=ROW_BUFS, align_bytes=64)
                 nc.sync.dma_start(out=rows[:], in_=sources[s][:, :, g0 * K_PASS : g1 * K_PASS])
                 raw[s, c] = rows[:].rearrange("q r k -> q (r k)").bitcast(F32).rearrange("q (r w) -> q r w", r=2)
 
         def sort_words(s, copy, n_passes):
             for c, (g0, g1) in enumerate(CHUNKS):
                 n = min(g1, n_passes) - g0
-                srt = work.tile([P, 2, 2, (g1 - g0) * P], F32, name="sorted%d" % c, bufs=2, align_bytes=64)
+                if n <= 0:
+                    continue
+                srt = work.tile([P, 2, 2, (g1 - g0) * P], F32, name="sorted%d" % c, bufs=3, align_bytes=64)
                 copy(out=srt[:, :, :, : n * P],
                      in_=raw[s, c][:, :, : n * WORDS].rearrange("q r (w u) -> q r u w", u=2))
                 for g in range(g0, g0 + n):
@@ -91,7 +96,7 @@ def tile_attention_pa_kernel(tc, x, wq, wk, wv, out_0, out_1, out_2):
             copy(out=words, in_=banks[s, g][:].rearrange("q r u c -> q r c u"))
 
         def quantise(s, part):
-            is_x = s < 2
+            is_x = s in (0, 2)
             if part == 0:
                 tag = "x" if is_x else "w"
                 codes[s] = work.tile([P, PASSES, SLAB], U32, name=tag + "_codes", bufs=2 if is_x else 3, align_bytes=64)
@@ -102,35 +107,35 @@ def tile_attention_pa_kernel(tc, x, wq, wk, wv, out_0, out_1, out_2):
                 scales=scales[s][:, g0:g1, :].rearrange("q g c -> q (g c)"),
                 in_=grouped[s][:, g0:g1, :].rearrange("q g c -> q (g c)"))
 
-        def matmuls(n):
-            for jp in range(2):
-                acc = psum.tile([P, 2 * SLAB], F32, name="acc", bufs=3)
-                for j in range(2):
-                    for g in range(PASSES):
-                        nc.tensor.matmul_mx(
-                            out=acc[:, j * SLAB : (j + 1) * SLAB],
-                            lhsT=codes[jp][:, g, j * P : (j + 1) * P].bitcast(E5M2),
-                            lhsT_scale=scales[jp][:, g, j * P : (j + 1) * P],
-                            rhs=codes[n + 2][:, g, :].bitcast(E4M3),
-                            rhs_scale=scales[n + 2][:, g, :],
-                            start=(g == 0), stop=(g == PASSES - 1))
-                accs[n, jp] = acc
+        def matmuls(n, j0, j1):
+            acc = psum.tile([P, 2 * SLAB], F32, name="acc", bufs=3)
+            for j in range(j0, j1):
+                cols = slice(j % 2 * P, (j % 2 + 1) * P)
+                for g in range(PASSES):
+                    nc.tensor.matmul_mx(
+                        out=acc[:, (j - j0) * SLAB : (j - j0 + 1) * SLAB],
+                        lhsT=codes[x_slab[j]][:, g, cols].bitcast(E5M2),
+                        lhsT_scale=scales[x_slab[j]][:, g, cols],
+                        rhs=codes[w_slab[n]][:, g, :].bitcast(E4M3),
+                        rhs_scale=scales[w_slab[n]][:, g, :],
+                        start=(g == 0), stop=(g == PASSES - 1))
+            accs[n, j0] = acc
 
         def stage_tile(n):
             if n not in staged:
                 staged[n] = work.tile([P, 2, TOK, DH], F32, name="staged", bufs=4)
             return staged[n]
 
-        def copy_out(n, jp):
-            nc.scalar.copy(out=stage_tile(n)[:, :, 2 * jp : 2 * jp + 2, :].rearrange("q h j d -> q j h d"),
-                           in_=accs[n, jp][:].rearrange("q (j h d) -> q j h d", j=2, h=2))
+        def copy_out(n, j0, j1):
+            nc.scalar.copy(out=stage_tile(n)[:, :, j0:j1, :].rearrange("q h j d -> q j h d"),
+                           in_=accs[n, j0][:, : (j1 - j0) * SLAB].rearrange("q (j h d) -> q j h d", h=2, d=DH))
 
         def rope_products(n, jp):
             shape = [P, 2, 2, 4, HALF]
             prod = work.tile(shape, F32, name="prod", bufs=3)
             nc.vector.tensor_tensor(
                 out=prod[:],
-                in0=accs[n, jp][:].rearrange("q (o j a i) -> q o j a i", o=1, j=2, a=4).to_broadcast(shape),
+                in0=accs[n, 2 * jp][:].rearrange("q (o j a i) -> q o j a i", o=1, j=2, a=4).to_broadcast(shape),
                 in1=tables[steps[n][2]][:, jp].rearrange("q c j (o i) -> q c j o i", o=1).to_broadcast(shape),
                 op=ALU.mult)
             prods[n, jp] = prod
@@ -150,7 +155,7 @@ def tile_attention_pa_kernel(tc, x, wq, wk, wv, out_0, out_1, out_2):
         def is_rope(n):
             return 0 <= n < n_steps and steps[n][2] is not None
 
-        for s in range(HEAD_SLABS):
+        for s in range(ROW_BUFS):
             load(s)
 
         ident = const.tile([P, P], F32)
@@ -179,55 +184,63 @@ def tile_attention_pa_kernel(tc, x, wq, wk, wv, out_0, out_1, out_2):
         nc.scalar.activation(out=table_k[:].rearrange(flat), in_=rest[:], func=ACT.Sin, scale=2.0 * math.pi)
         tables = {"q": table_q, "k": table_k}
 
-        def head_slab(s):
-            transposes(s)
+        def gather_all(s):
             for g in range(PASSES):
-                gather(s, g, nc.vector.tensor_copy if g % 2 else nc.scalar.copy)
-            for part in range(len(QUANT)):
-                quantise(s, part)
+                gather(s, g, nc.vector.tensor_copy if s < HEAD_SLABS and g == PASSES - 1 else nc.scalar.copy)
+                if s < HEAD_SLABS and g == 1:
+                    quantise(s, 0)
 
         for s in range(3):
-            head_slab(s)
-            load(s + HEAD_SLABS)
-            if s == 0:
-                nc.vector.tensor_scalar(out=table_q[:].rearrange(flat), in0=table_k[:].rearrange(flat),
-                                        scalar1=Q_SCALE, scalar2=None, op0=ALU.mult)
+            transposes(s)
+            gather_all(s)
+            quantise(s, 1)
+            quantise(s, 2)
+            load(s + ROW_BUFS)
+        matmuls(0, 0, 2)
+        copy_out(0, 0, 2)
 
+        last = n_steps - 1
         for n in range(n_steps):
             s = n + 3
             more = s < n_slabs
             if more:
                 transposes(s)
+            if n < 3:
+                sort_words(s + 1, nc.vector.tensor_copy, PASSES)
             if n > 0:
                 if is_rope(n - 1):
                     rope_products(n - 1, 1)
                     rope_sums(n - 1, 0)
                 else:
-                    copy_out(n - 1, 1)
+                    copy_out(n - 1, 2, TOK)
             if more:
-                for g in range(PASSES):
-                    gather(s, g, nc.vector.tensor_copy if s < HEAD_SLABS and g % 2 else nc.scalar.copy)
-                quantise(s, 0)
+                gather_all(s)
+                if s >= HEAD_SLABS:
+                    quantise(s, 0)
             if is_rope(n - 1):
                 rope_sums(n - 1, 1)
             if n > 0:
                 store(n - 1, 0, TOK)
-            if s + HEAD_SLABS < n_slabs:
-                load(s + HEAD_SLABS)
+            if s + ROW_BUFS < n_slabs:
+                load(s + ROW_BUFS)
             if more:
                 quantise(s, 1)
                 quantise(s, 2)
-            matmuls(n)
-            if is_rope(n):
-                rope_products(n, 0)
-            else:
-                copy_out(n, 0)
-            if s + 1 < n_slabs:
-                if is_rope(n - 1):
-                    sort_words(s + 1, nc.scalar.copy, SORTED_BY_SCALAR)
+            if n == 1:
+                nc.vector.tensor_scalar(out=table_q[:].rearrange(flat), in0=table_k[:].rearrange(flat),
+                                        scalar1=Q_SCALE, scalar2=None, op0=ALU.mult)
+            if n > 0:
+                matmuls(n, 0, 2)
+                if is_rope(n):
+                    rope_products(n, 0)
                 else:
-                    sort_words(s + 1, nc.vector.tensor_copy, PASSES)
-        last = n_steps - 1
+                    copy_out(n, 0, 2)
+            if n < last:
+                matmuls(n, 2, TOK)
+            if n >= 2 and s + 2 < n_slabs:
+                sort_words(s + 2, nc.scalar.copy, SORTED_BY_SCALAR)
         store(last, 0, 2)
-        copy_out(last, 1)
-        store(last, 2, TOK)
+        for j in range(2, TOK):
+            matmuls(last, j, j + 1)
+            copy_out(last, j, j + 1)
+            store(last, j, j + 1)

import math
from contextlib import ExitStack

import concourse.mybir as mybir
from concourse.masks import make_identity

L, D, H, G, DH = 512, 2560, 16, 8, 128
HALF = DH // 2
ROPE_THETA = 10000.0
Q_SCALE = 1.0 / math.sqrt(144.0)
FLOPS = 2 * L * D * (H + 2 * G) * DH

F32 = mybir.dt.float32
BF16 = mybir.dt.bfloat16
I32 = mybir.dt.int32
U32 = mybir.dt.uint32
U8 = mybir.dt.uint8
E4M3 = mybir.dt.float8_e4m3fn_x4
E5M2 = mybir.dt.float8_e5m2_x4
ALU = mybir.AluOpType
ACT = mybir.ActivationFunctionType

P = 128
K_PASS = 512
PASSES = D // K_PASS
WORDS = K_PASS // 2
SLAB = 256
TOK = L // P
CHUNKS = ((0, 3), (3, 5))
QUANT = ((0, 2), (2, 4), (4, 5))
HEAD_SLABS = 4
ROW_BUFS = 5
SORTED_BY_SCALAR = 4


def tile_attention_pa_kernel(tc, x, wq, wk, wv, out_0, out_1, out_2):
    nc = tc.nc
    x_rows = x[0].rearrange("(p j) k -> p j k", j=TOK)

    def weight_slabs(w, out, table, first, last):
        return [(w[SLAB * m : SLAB * (m + 1), :].rearrange("(r p) k -> p r k", p=P),
                 out[0, 2 * m : 2 * m + 2].rearrange("h (p j) d -> p h (j d)", j=TOK), table)
                for m in range(first, last)]

    v_slabs = G // 2
    steps = (weight_slabs(wv, out_2, None, 0, v_slabs // 2) + weight_slabs(wq, out_0, "q", 0, H // 2)
             + weight_slabs(wk, out_1, "k", 0, G // 2) + weight_slabs(wv, out_2, None, v_slabs // 2, v_slabs))
    n_steps = len(steps)
    sources = [x_rows[:, 0:2, :], steps[0][0], x_rows[:, 2:4, :]] + [step[0] for step in steps[1:]]
    x_slab = {0: 0, 1: 0, 2: 2, 3: 2}
    w_slab = [1] + list(range(3, n_steps + 2))
    n_slabs = len(sources)

    with ExitStack() as ctx:
        const = ctx.enter_context(tc.tile_pool(name="const", bufs=1))
        work = ctx.enter_context(tc.tile_pool(name="work", bufs=3))
        psum = ctx.enter_context(tc.psum_pool(name="psum", bufs=1))
        ctx.enter_context(tc.manual_schedule())

        raw, ordered, banks, grouped, codes, scales, accs, prods, staged = {}, {}, {}, {}, {}, {}, {}, {}, {}

        def load(s):
            for c, (g0, g1) in enumerate(CHUNKS):
                rows = work.tile([P, 2, (g1 - g0) * K_PASS], BF16, name="rows%d" % c, bufs=ROW_BUFS, align_bytes=64)
                nc.sync.dma_start(out=rows[:], in_=sources[s][:, :, g0 * K_PASS : g1 * K_PASS])
                raw[s, c] = rows[:].rearrange("q r k -> q (r k)").bitcast(F32).rearrange("q (r w) -> q r w", r=2)

        def sort_words(s, copy, n_passes):
            for c, (g0, g1) in enumerate(CHUNKS):
                n = min(g1, n_passes) - g0
                if n <= 0:
                    continue
                srt = work.tile([P, 2, 2, (g1 - g0) * P], F32, name="sorted%d" % c, bufs=3, align_bytes=64)
                copy(out=srt[:, :, :, : n * P],
                     in_=raw[s, c][:, :, : n * WORDS].rearrange("q r (w u) -> q r u w", u=2))
                for g in range(g0, g0 + n):
                    ordered[s, g] = srt[:, :, :, (g - g0) * P : (g - g0 + 1) * P]

        def transposes(s):
            for c, (g0, g1) in enumerate(CHUNKS):
                for g in range(g0, g1):
                    bank = psum.tile([P, 2, 2, P], F32, name="turned", bufs=5)
                    for r in range(2):
                        for u in range(2):
                            if (s, g) in ordered:
                                src = ordered[s, g][:, r, u, :]
                            else:
                                src = raw[s, c][:, r, (g - g0) * WORDS + u : (g - g0 + 1) * WORDS : 2]
                            nc.tensor.transpose(bank[:, r, u, :], src, ident[:])
                    banks[s, g] = bank

        def gather(s, g, copy):
            if g == 0:
                grouped[s] = work.tile([P, PASSES, 4 * SLAB], BF16, name="grouped", bufs=2, align_bytes=64)
            words = grouped[s][:, g, :].bitcast(F32).rearrange("q (r c u) -> q r c u", r=2, u=2)
            copy(out=words, in_=banks[s, g][:].rearrange("q r u c -> q r c u"))

        def quantise(s, part):
            is_x = s in (0, 2)
            if part == 0:
                tag = "x" if is_x else "w"
                codes[s] = work.tile([P, PASSES, SLAB], U32, name=tag + "_codes", bufs=2 if is_x else 3, align_bytes=64)
                scales[s] = work.tile([P, PASSES, SLAB], U8, name=tag + "_scales", bufs=2 if is_x else 3, align_bytes=64)
            g0, g1 = QUANT[part]
            nc.vector.quantize_mx(
                out=codes[s][:, g0:g1, :].rearrange("q g c -> q (g c)").bitcast(E5M2 if is_x else E4M3),
                scales=scales[s][:, g0:g1, :].rearrange("q g c -> q (g c)"),
                in_=grouped[s][:, g0:g1, :].rearrange("q g c -> q (g c)"))

        def matmuls(n, j0, j1):
            acc = psum.tile([P, 2 * SLAB], F32, name="acc", bufs=3)
            for j in range(j0, j1):
                cols = slice(j % 2 * P, (j % 2 + 1) * P)
                for g in range(PASSES):
                    nc.tensor.matmul_mx(
                        out=acc[:, (j - j0) * SLAB : (j - j0 + 1) * SLAB],
                        lhsT=codes[x_slab[j]][:, g, cols].bitcast(E5M2),
                        lhsT_scale=scales[x_slab[j]][:, g, cols],
                        rhs=codes[w_slab[n]][:, g, :].bitcast(E4M3),
                        rhs_scale=scales[w_slab[n]][:, g, :],
                        start=(g == 0), stop=(g == PASSES - 1))
            accs[n, j0] = acc

        def stage_tile(n):
            if n not in staged:
                staged[n] = work.tile([P, 2, TOK, DH], F32, name="staged", bufs=4)
            return staged[n]

        def copy_out(n, j0, j1):
            nc.scalar.copy(out=stage_tile(n)[:, :, j0:j1, :].rearrange("q h j d -> q j h d"),
                           in_=accs[n, j0][:, : (j1 - j0) * SLAB].rearrange("q (j h d) -> q j h d", h=2, d=DH))

        def rope_products(n, jp):
            shape = [P, 2, 2, 4, HALF]
            prod = work.tile(shape, F32, name="prod", bufs=3)
            nc.vector.tensor_tensor(
                out=prod[:],
                in0=accs[n, 2 * jp][:].rearrange("q (o j a i) -> q o j a i", o=1, j=2, a=4).to_broadcast(shape),
                in1=tables[steps[n][2]][:, jp].rearrange("q c j (o i) -> q c j o i", o=1).to_broadcast(shape),
                op=ALU.mult)
            prods[n, jp] = prod

        def rope_sums(n, jp):
            dst = stage_tile(n)[:, :, 2 * jp : 2 * jp + 2, :].rearrange("q h j (a i) -> q j h a i", a=2)
            prod = prods[n, jp][:].rearrange("q c j (h a) i -> q c j h a i", a=2)
            nc.vector.tensor_tensor(out=dst[:, :, :, 0, :], in0=prod[:, 0, :, :, 0, :], in1=prod[:, 1, :, :, 1, :],
                                    op=ALU.subtract)
            nc.vector.tensor_tensor(out=dst[:, :, :, 1, :], in0=prod[:, 0, :, :, 1, :], in1=prod[:, 1, :, :, 0, :],
                                    op=ALU.add)

        def store(n, j0, j1):
            nc.sync.dma_start(out=steps[n][1][:, :, j0 * DH : j1 * DH],
                              in_=staged[n][:, :, j0:j1, :].rearrange("q h j d -> q h (j d)"))

        def is_rope(n):
            return 0 <= n < n_steps and steps[n][2] is not None

        for s in range(ROW_BUFS):
            load(s)

        ident = const.tile([P, P], F32)
        pos = const.tile([P, TOK], F32)
        nc.gpsimd.iota(pos[:], [[1, TOK]], base=0, channel_multiplier=TOK, allow_small_or_imprecise_dtypes=True)
        make_identity(nc, ident[:])

        turns = const.tile([P, 2, 2, 2, HALF], F32)
        ratio = ROPE_THETA ** (-1.0 / HALF)
        pos_view = pos[:].rearrange("q (t j o) -> q t j o", t=2, o=1)
        for i in range(8):
            nc.vector.tensor_scalar(out=turns[:, :, 1, :, i : i + 1], in0=pos_view,
                                    scalar1=ratio**i / (2.0 * math.pi), scalar2=None, op0=ALU.mult)
        for b in range(1, 8):
            nc.vector.tensor_scalar(out=turns[:, :, 1, :, 8 * b : 8 * b + 8], in0=turns[:, :, 1, :, 0:8],
                                    scalar1=ratio ** (8 * b), scalar2=None, op0=ALU.mult)
        nc.vector.tensor_scalar(out=turns[:, :, 0, :, :], in0=turns[:, :, 1, :, :],
                                scalar1=0.25, scalar2=None, op0=ALU.add)
        flat = "q t c j i -> q (t c j i)"
        whole = const.tile([P, 8 * HALF], I32)
        nc.vector.tensor_copy(out=whole[:], in_=turns[:].rearrange(flat))
        rest = const.tile([P, 8 * HALF], F32)
        nc.vector.tensor_tensor(out=rest[:], in0=turns[:].rearrange(flat), in1=whole[:], op=ALU.subtract)
        table_k = const.tile([P, 2, 2, 2, HALF], F32)
        table_q = const.tile([P, 2, 2, 2, HALF], F32)
        nc.scalar.activation(out=table_k[:].rearrange(flat), in_=rest[:], func=ACT.Sin, scale=2.0 * math.pi)
        tables = {"q": table_q, "k": table_k}

        def gather_all(s):
            for g in range(PASSES):
                gather(s, g, nc.vector.tensor_copy if s < HEAD_SLABS and g == PASSES - 1 else nc.scalar.copy)
                if s < HEAD_SLABS and g == 1:
                    quantise(s, 0)

        for s in range(3):
            transposes(s)
            gather_all(s)
            quantise(s, 1)
            quantise(s, 2)
            load(s + ROW_BUFS)
        matmuls(0, 0, 2)
        copy_out(0, 0, 2)

        last = n_steps - 1
        for n in range(n_steps):
            s = n + 3
            more = s < n_slabs
            if more:
                transposes(s)
            if n < 3:
                sort_words(s + 1, nc.vector.tensor_copy, PASSES)
            if n > 0:
                if is_rope(n - 1):
                    rope_products(n - 1, 1)
                    rope_sums(n - 1, 0)
                else:
                    copy_out(n - 1, 2, TOK)
            if more:
                gather_all(s)
                if s >= HEAD_SLABS:
                    quantise(s, 0)
            if is_rope(n - 1):
                rope_sums(n - 1, 1)
            if n > 0:
                store(n - 1, 0, TOK)
            if s + ROW_BUFS < n_slabs:
                load(s + ROW_BUFS)
            if more:
                quantise(s, 1)
                quantise(s, 2)
            if n == 1:
                nc.vector.tensor_scalar(out=table_q[:].rearrange(flat), in0=table_k[:].rearrange(flat),
                                        scalar1=Q_SCALE, scalar2=None, op0=ALU.mult)
            if n > 0:
                matmuls(n, 0, 2)
                if is_rope(n):
                    rope_products(n, 0)
                else:
                    copy_out(n, 0, 2)
            if n < last:
                matmuls(n, 2, TOK)
            if n >= 2 and s + 2 < n_slabs:
                sort_words(s + 2, nc.scalar.copy, SORTED_BY_SCALAR)
        store(last, 0, 2)
        for j in range(2, TOK):
            matmuls(last, j, j + 1)
            copy_out(last, j, j + 1)
            store(last, j, j + 1)
